import numpy as np
import ml_dtypes


def mxq(x, axis, fmt="e4m3"):
    dtype, down = {"e4m3": (ml_dtypes.float8_e4m3fn, 7), "e5m2": (ml_dtypes.float8_e5m2, 14)}[fmt]
    v = np.moveaxis(np.asarray(x, np.float32).astype(ml_dtypes.bfloat16).astype(np.float64), axis, -1)
    blocks = v.reshape(v.shape[:-1] + (-1, 32))
    amax = np.abs(blocks).max(-1, keepdims=True)
    byte = np.maximum(np.where(amax > 0, np.frexp(amax)[1] - 1 + 127, 0) - down, 1)
    scale = np.exp2(byte - 127.0)
    codes = (blocks / scale).astype(np.float32).astype(dtype).astype(np.float64)
    return np.moveaxis((codes * scale).reshape(v.shape), -1, axis)


WIDE = False


def mx_kscale(k):
    if not WIDE:
        return np.ones(k)
    levels = np.array([10, -10, 5, -5, 0])
    a = np.random.permutation(np.resize(levels, k // 512 * 4)).reshape(k // 512, 4)
    idx = np.arange(k)
    return np.exp2(a[idx // 512, idx % 128 // 32])


BF16 = ml_dtypes.bfloat16


def bf(x):
    return np.asarray(x, np.float32).astype(BF16)


def f64(x):
    return np.asarray(x).astype(np.float64)


E2M1 = np.array([0.0, 0.5, 1.0, 1.5, 2.0, 3.0, 4.0, 6.0, -0.0, -0.5, -1.0, -1.5, -2.0, -3.0, -4.0, -6.0])


def pack_weight(w, fmt):
    k, n = w.shape
    w = f64(bf(w)).reshape(k // 32, 32, n)
    amax = np.abs(w).max(1)
    if fmt == "e4m3":
        byte = np.frexp(amax)[1] - 1 + 127 - 7
    else:
        mant, ex = np.frexp(amax / 6.0)
        byte = np.where(mant > 0.5, ex, ex - 1) + 127
    byte = np.clip(np.where(amax > 0, byte, 1), 1, 254)
    scaled = (w * np.exp2(127.0 - byte)[:, None, :]).reshape(k, n).astype(np.float32)
    by_word = np.ascontiguousarray(scaled.reshape(k // 512, 128, 4, n).transpose(0, 1, 3, 2))
    if fmt == "e4m3":
        words = by_word.astype(ml_dtypes.float8_e4m3fn).view(np.uint8)
    else:
        c = by_word.astype(ml_dtypes.float4_e2m1fn).view(np.uint8) & 0xF
        words = c[..., 0::2] | (c[..., 1::2] << 4)
    return np.ascontiguousarray(words), np.ascontiguousarray(byte.astype(np.uint8).reshape(k // 512, 16, n))


def unpack_weight(words, scales, fmt):
    g, p, n, _ = words.shape
    if fmt == "e4m3":
        vals = np.ascontiguousarray(words).view(ml_dtypes.float8_e4m3fn).astype(np.float64)
    else:
        nib = np.empty((g, p, n, 4), np.uint8)
        nib[..., 0::2] = words & 0xF
        nib[..., 1::2] = words >> 4
        vals = E2M1[nib]
    vals = vals * np.repeat(np.exp2(scales.astype(np.float64) - 127.0), 8, axis=1)[..., None]
    return vals.transpose(0, 1, 3, 2).reshape(g * 512, n)

def pack4(w):
    words, scales = pack_weight(w, "e2m1")
    return words.reshape(words.shape[0], 128, -1), scales


def unpack4(words, scales):
    return unpack_weight(words.reshape(words.shape[0], 128, -1, 2), scales, "e2m1")


IN, H, C, B = 1024, 256, 2, 4096
QH = H % 512 == 0


def sigmoid(v):
    return 1.0 / (1.0 + np.exp(-v))


def setup_inputs():
    s = mx_kscale(IN)
    t = mx_kscale(H) if QH else np.ones(H)
    input_word = bf(np.random.standard_normal((B, IN)) * s)
    hidden_states = bf(np.random.standard_normal((B, H)) * t)
    wx = np.random.uniform(-1.0, 1.0, (C, 2 * H, IN)) / np.sqrt(IN) / s
    cat = np.ascontiguousarray(wx.swapaxes(1, 2)).reshape(-1, 2 * H)
    words, scales = pack4(cat)
    bx = bf(np.random.standard_normal((C, 2 * H)) * 0.3)
    Wh = bf(np.random.uniform(-1.0, 1.0, (C, 2 * H, H)) / np.sqrt(H) / t)
    return {"input_word": input_word,
            "hidden_states": hidden_states,
            "Wx_words": words,
            "Wx_scales": scales,
            "bx": bx,
            "Wh": Wh}


def reference(input_word, hidden_states, Wx_words, Wx_scales, bx, Wh):
    px = mxq(f64(input_word), 1, "e4m3") @ unpack4(Wx_words, Wx_scales).reshape(C, IN, 2 * H)
    if QH:
        ph = mxq(f64(hidden_states), 1, "e4m3") @ mxq(f64(Wh), 2, "e4m3").transpose(0, 2, 1)
    else:
        ph = f64(hidden_states) @ f64(Wh).transpose(0, 2, 1)
    net = px.transpose(1, 0, 2) + ph.transpose(1, 0, 2) + f64(bx)[None, :, :]
    input_gate, cell_states = net[..., :H], net[..., H:]
    cell_input = np.tanh(cell_states)
    input_gate = sigmoid(input_gate)
    return (cell_input, input_gate)

@@ -1,0 +1,208 @@
+from contextlib import ExitStack
+
+import concourse.mybir as mybir
+from concourse.masks import make_identity
+
+F32 = mybir.dt.float32
+BF16 = mybir.dt.bfloat16
+I32 = mybir.dt.int32
+U32 = mybir.dt.uint32
+U8 = mybir.dt.uint8
+FP8X4 = mybir.dt.float8_e4m3fn_x4
+FP4X4 = mybir.dt.float4_e2m1fn_x4
+ADD = mybir.AluOpType.add
+SIGMOID = mybir.ActivationFunctionType.Sigmoid
+TANH = mybir.ActivationFunctionType.Tanh
+
+P = 128
+BATCH, IN, HID, CELLS = 4096, 1024, 256, 2
+NET = 2 * HID
+PACK = 4
+K_PASS = P * PACK
+PASSES = IN // K_PASS
+GROUPS = CELLS * PASSES
+K_TILES = HID // P
+TILES = BATCH // P
+ROUND = 2
+ROUNDS = TILES // ROUND
+LOOKAHEAD = 4
+
+FLOPS = 2 * BATCH * CELLS * NET * (IN + HID)
+
+
+def tile_compute_gate_t_e_kernel(
+    tc, input_word, hidden_states, Wx_words, Wx_scales, bx, Wh, out_0, out_1
+):
+    nc = tc.nc
+    x_rows = input_word.rearrange("(p t) k -> p t k", t=TILES)
+    h_rows = hidden_states.rearrange("(p t) k -> p t k", t=TILES)
+    cell_rows = out_0.rearrange("(p t) c n -> p t c n", t=TILES)
+    gate_rows = out_1.rearrange("(p t) c n -> p t c n", t=TILES)
+
+    with ExitStack() as ctx:
+        ctx.enter_context(tc.manual_schedule())
+        consts = ctx.enter_context(tc.tile_pool(name="consts", bufs=1))
+        stream = ctx.enter_context(tc.tile_pool(name="stream", bufs=LOOKAHEAD + 1))
+        work = ctx.enter_context(tc.tile_pool(name="work", bufs=2 * ROUND))
+        results = ctx.enter_context(tc.tile_pool(name="results", bufs=4))
+        psum = ctx.enter_context(tc.psum_pool(name="psum", bufs=1))
+
+        x_tiles, h_tiles = {}, {}
+        grouped_tiles, code_tiles, plane_tiles = {}, {}, {}
+        ht_tiles = {}
+
+        def load_round(j):
+            first = j * ROUND
+            x_sb = stream.tile([P, ROUND, IN], BF16)
+            nc.sync.dma_start(out=x_sb[:], in_=x_rows[:, first : first + ROUND, :])
+            h_sb = stream.tile([P, ROUND, HID], BF16)
+            nc.sync.dma_start(out=h_sb[:], in_=h_rows[:, first : first + ROUND, :])
+            x_tiles[j], h_tiles[j] = x_sb, h_sb
+
+        def transpose_round(j):
+            for i in range(ROUND):
+                words = x_tiles[j][:, i, :].bitcast(F32)
+                xt = psum.tile([P, PASSES * 2, P], F32, tag="xt", bufs=ROUND)
+                for g in range(PASSES):
+                    for u in range(2):
+                        nc.tensor.transpose(
+                            xt[:, 2 * g + u, :],
+                            words[:, 256 * g + u : 256 * (g + 1) : 2],
+                            ident_f32[:],
+                        )
+                grouped = work.tile([P, PASSES, P, PACK], BF16, align_bytes=64)
+                nc.scalar.copy(
+                    out=grouped[:].bitcast(F32),
+                    in_=xt[:].rearrange("p (g u) r -> p g r u", u=2),
+                )
+                grouped_tiles[(j, i)] = grouped
+            ht = psum.tile([P, ROUND, K_TILES, P], BF16, tag="ht", bufs=1)
+            for i in range(ROUND):
+                for kt in range(K_TILES):
+                    nc.tensor.transpose(
+                        ht[:, i, kt, :], h_tiles[j][:, i, kt * P : (kt + 1) * P], ident_bf16[:]
+                    )
+            ht_sb = work.tile([P, ROUND, K_TILES, P], BF16)
+            nc.scalar.copy(out=ht_sb[:], in_=ht[:])
+            ht_tiles[j] = ht_sb
+
+        def quantise_tile(j, i):
+            codes = work.tile([P, PASSES * P], U32, align_bytes=64)
+            planes = work.tile([P, PASSES * P], U8, align_bytes=64)
+            nc.vector.quantize_mx(
+                out=codes[:].bitcast(FP8X4),
+                scales=planes[:],
+                in_=grouped_tiles[(j, i)][:].rearrange("p g r t -> p (g r t)"),
+            )
+            code_tiles[(j, i)], plane_tiles[(j, i)] = codes, planes
+
+        def gates_tile(j, i):
+            codes, planes, ht_sb = code_tiles[(j, i)], plane_tiles[(j, i)], ht_tiles[j]
+            hidden_products, mx_products = [], []
+            for c in range(CELLS):
+                ph = psum.tile([P, NET], F32, tag="ph", bufs=2)
+                for kt in range(K_TILES):
+                    nc.tensor.matmul(
+                        ph[:],
+                        lhsT=ht_sb[:, i, kt, :],
+                        rhs=wh_t[:, kt, c * NET : (c + 1) * NET],
+                        start=(kt == 0),
+                        stop=(kt == K_TILES - 1),
+                    )
+                hidden_products.append(ph)
+            for c in range(CELLS):
+                px = psum.tile([P, NET], F32, tag="px", bufs=3)
+                for g in range(PASSES):
+                    nc.tensor.matmul_mx(
+                        out=px[:],
+                        lhsT=codes[:, g * P : (g + 1) * P].bitcast(FP8X4),
+                        lhsT_scale=planes[:, g * P : (g + 1) * P],
+                        rhs=w_words[:, c * PASSES + g, :].bitcast(FP4X4),
+                        rhs_scale=w_planes[:, c * PASSES + g, :],
+                        start=(g == 0),
+                        stop=(g == PASSES - 1),
+                    )
+                mx_products.append(px)
+            net = results.tile([P, CELLS, NET], F32)
+            for c in range(CELLS):
+                nc.vector.tensor_tensor(
+                    out=net[:, c, :], in0=hidden_products[c][:], in1=bias[:, c, :], op=ADD
+                )
+            for c in range(CELLS):
+                nc.vector.tensor_tensor(
+                    out=net[:, c, :], in0=mx_products[c][:], in1=net[:, c, :], op=ADD
+                )
+            t = j * ROUND + i
+            gate = results.tile([P, CELLS, HID], F32)
+            nc.scalar.activation(out=gate[:], in_=net[:, :, 0:HID], func=SIGMOID)
+            nc.sync.dma_start(out=gate_rows[:, t, :, :], in_=gate[:])
+            cell = results.tile([P, CELLS, HID], F32)
+            nc.scalar.activation(out=cell[:], in_=net[:, :, HID:NET], func=TANH)
+            nc.sync.dma_start(out=cell_rows[:, t, :, :], in_=cell[:])
+
+        ident_f32 = consts.tile([P, P], F32)
+        make_identity(nc, ident_f32[:])
+        ident_bf16 = consts.tile([P, P], BF16)
+        make_identity(nc, ident_bf16[:])
+        ones = consts.tile([P, P], BF16)
+        nc.vector.memset(ones[:], 1.0)
+        bias_row = consts.tile([P, CELLS * NET], BF16)
+        nc.vector.memset(bias_row[:], 0.0)
+        w_planes = consts.tile([P, GROUPS, NET], U8, align_bytes=64)
+        nc.vector.memset(w_planes[:].rearrange("p g n -> p (g n)").bitcast(I32), 0)
+
+        load_round(0)
+        nc.sync.dma_start(out=bias_row[0:1, :], in_=bx.rearrange("(o c) n -> o (c n)", o=1))
+        for quadrant in range(4):
+            nc.sync.dma_start(
+                out=w_planes[32 * quadrant : 32 * quadrant + 4, :, :].bitcast(I32),
+                in_=Wx_scales[:, 4 * quadrant : 4 * quadrant + 4, :]
+                .rearrange("g r n -> r g n")
+                .bitcast(I32),
+            )
+        wh_rows = consts.tile([P, CELLS * NET // P, HID], BF16)
+        nc.sync.dma_start(out=wh_rows[:], in_=Wh.rearrange("c (b p) k -> p (c b) k", p=P))
+        w_words = consts.tile([P, GROUPS, 2 * NET], U8, align_bytes=64)
+        nc.sync.dma_start(
+            out=w_words[:].bitcast(I32), in_=Wx_words.rearrange("g p b -> p g b").bitcast(I32)
+        )
+        for j in range(1, LOOKAHEAD):
+            load_round(j)
+
+        bias = consts.tile([P, CELLS, NET], F32)
+        for c in range(CELLS):
+            spread = psum.tile([P, NET], F32, tag="px", bufs=3)
+            nc.tensor.matmul(
+                spread[:],
+                lhsT=ones[:],
+                rhs=bias_row[:, c * NET : (c + 1) * NET],
+                start=True,
+                stop=True,
+            )
+            nc.vector.tensor_copy(out=bias[:, c, :], in_=spread[:])
+
+        transpose_round(0)
+
+        wh_t = consts.tile([P, K_TILES, CELLS * NET], BF16)
+        for kt in range(K_TILES):
+            flipped = psum.tile([P, CELLS * NET], BF16, tag="ph", bufs=2)
+            for b in range(CELLS * NET // P):
+                nc.tensor.transpose(
+                    flipped[:, b * P : (b + 1) * P],
+                    wh_rows[:, b, kt * P : (kt + 1) * P],
+                    ident_bf16[:],
+                )
+            nc.vector.tensor_copy(out=wh_t[:, kt, :], in_=flipped[:])
+
+        for i in range(ROUND):
+            quantise_tile(0, i)
+
+        for j in range(ROUNDS):
+            if j + LOOKAHEAD < ROUNDS:
+                load_round(j + LOOKAHEAD)
+            if j + 1 < ROUNDS:
+                transpose_round(j + 1)
+            for i in range(ROUND):
+                gates_tile(j, i)
+                if j + 1 < ROUNDS:
+                    quantise_tile(j + 1, i)

@@ -23,9 +23,11 @@ PASSES = IN // K_PASS
 GROUPS = CELLS * PASSES
 K_TILES = HID // P
 TILES = BATCH // P
-ROUND = 2
-ROUNDS = TILES // ROUND
-LOOKAHEAD = 4
+LOAD = 2
+LOADS = TILES // LOAD
+LOADS_AHEAD = 4
+FLIP_AHEAD = 3
+HIDDEN_AHEAD = 1
 
 FLOPS = 2 * BATCH * CELLS * NET * (IN + HID)
 
@@ -42,74 +44,88 @@ def tile_compute_gate_t_e_kernel(
     with ExitStack() as ctx:
         ctx.enter_context(tc.manual_schedule())
         consts = ctx.enter_context(tc.tile_pool(name="consts", bufs=1))
-        stream = ctx.enter_context(tc.tile_pool(name="stream", bufs=LOOKAHEAD + 1))
-        work = ctx.enter_context(tc.tile_pool(name="work", bufs=2 * ROUND))
+        stream = ctx.enter_context(tc.tile_pool(name="stream", bufs=LOADS_AHEAD + 2))
+        work = ctx.enter_context(tc.tile_pool(name="work", bufs=FLIP_AHEAD + 1))
         results = ctx.enter_context(tc.tile_pool(name="results", bufs=4))
         psum = ctx.enter_context(tc.psum_pool(name="psum", bufs=1))
 
         x_tiles, h_tiles = {}, {}
-        grouped_tiles, code_tiles, plane_tiles = {}, {}, {}
-        ht_tiles = {}
+        xt_tiles, ht_tiles = {}, {}
+        grouped_tiles, code_tiles, plane_tiles, ht_sb_tiles = {}, {}, {}, {}
+        ph_tiles, px_tiles, net_tiles = {}, {}, {}
 
-        def load_round(j):
-            first = j * ROUND
-            x_sb = stream.tile([P, ROUND, IN], BF16)
-            nc.sync.dma_start(out=x_sb[:], in_=x_rows[:, first : first + ROUND, :])
-            h_sb = stream.tile([P, ROUND, HID], BF16)
-            nc.sync.dma_start(out=h_sb[:], in_=h_rows[:, first : first + ROUND, :])
+        def load(j):
+            first = j * LOAD
+            x_sb = stream.tile([P, LOAD, IN], BF16)
+            nc.sync.dma_start(out=x_sb[:], in_=x_rows[:, first : first + LOAD, :])
+            h_sb = stream.tile([P, LOAD, HID], BF16)
+            nc.sync.dma_start(out=h_sb[:], in_=h_rows[:, first : first + LOAD, :])
             x_tiles[j], h_tiles[j] = x_sb, h_sb
 
-        def transpose_round(j):
-            for i in range(ROUND):
-                words = x_tiles[j][:, i, :].bitcast(F32)
-                xt = psum.tile([P, PASSES * 2, P], F32, tag="xt", bufs=ROUND)
-                for g in range(PASSES):
-                    for u in range(2):
-                        nc.tensor.transpose(
-                            xt[:, 2 * g + u, :],
-                            words[:, 256 * g + u : 256 * (g + 1) : 2],
-                            ident_f32[:],
-                        )
-                grouped = work.tile([P, PASSES, P, PACK], BF16, align_bytes=64)
-                nc.scalar.copy(
-                    out=grouped[:].bitcast(F32),
-                    in_=xt[:].rearrange("p (g u) r -> p g r u", u=2),
-                )
-                grouped_tiles[(j, i)] = grouped
-            ht = psum.tile([P, ROUND, K_TILES, P], BF16, tag="ht", bufs=1)
-            for i in range(ROUND):
-                for kt in range(K_TILES):
-                    nc.tensor.transpose(
-                        ht[:, i, kt, :], h_tiles[j][:, i, kt * P : (kt + 1) * P], ident_bf16[:]
-                    )
-            ht_sb = work.tile([P, ROUND, K_TILES, P], BF16)
-            nc.scalar.copy(out=ht_sb[:], in_=ht[:])
-            ht_tiles[j] = ht_sb
+        def flip_x(t, s):
+            if s == 0:
+                xt = psum.tile([P, PASSES * 2, P], F32, tag="xt", bufs=2)
+                xt_tiles[t] = xt
+            g, u = divmod(s, 2)
+            words = x_tiles[t // LOAD][:, t % LOAD, :].bitcast(F32)
+            nc.tensor.transpose(
+                xt_tiles[t][:, s, :], words[:, 256 * g + u : 256 * (g + 1) : 2], ident_f32[:]
+            )
 
-        def quantise_tile(j, i):
+        def flip_h(t, kt):
+            if kt == 0:
+                ht = psum.tile([P, K_TILES, P], BF16, tag="ht", bufs=1)
+                ht_tiles[t] = ht
+            nc.tensor.transpose(
+                ht_tiles[t][:, kt, :],
+                h_tiles[t // LOAD][:, t % LOAD, kt * P : (kt + 1) * P],
+                ident_bf16[:],
+            )
+
+        def hidden_pass(t, s):
+            c, kt = divmod(s, K_TILES)
+            if kt == 0:
+                ph = psum.tile([P, NET], F32, tag="ph", bufs=2)
+                ph_tiles[(t, c)] = ph
+            nc.tensor.matmul(
+                ph_tiles[(t, c)][:],
+                lhsT=ht_sb_tiles[t][:, kt, :],
+                rhs=wh_t[:, kt, c * NET : (c + 1) * NET],
+                start=(kt == 0),
+                stop=(kt == K_TILES - 1),
+            )
+
+        def copy_flipped(t):
+            grouped = work.tile([P, PASSES, P, PACK], BF16, align_bytes=64)
+            nc.scalar.copy(
+                out=grouped[:].bitcast(F32),
+                in_=xt_tiles[t][:].rearrange("p (g u) r -> p g r u", u=2),
+            )
+            grouped_tiles[t] = grouped
+            ht_sb = work.tile([P, K_TILES, P], BF16)
+            nc.scalar.copy(out=ht_sb[:], in_=ht_tiles[t][:])
+            ht_sb_tiles[t] = ht_sb
+
+        def quantise(t):
             codes = work.tile([P, PASSES * P], U32, align_bytes=64)
             planes = work.tile([P, PASSES * P], U8, align_bytes=64)
             nc.vector.quantize_mx(
                 out=codes[:].bitcast(FP8X4),
                 scales=planes[:],
-                in_=grouped_tiles[(j, i)][:].rearrange("p g r t -> p (g r t)"),
+                in_=grouped_tiles[t][:].rearrange("p g r t -> p (g r t)"),
             )
-            code_tiles[(j, i)], plane_tiles[(j, i)] = codes, planes
+            code_tiles[t], plane_tiles[t] = codes, planes
 
-        def gates_tile(j, i):
-            codes, planes, ht_sb = code_tiles[(j, i)], plane_tiles[(j, i)], ht_tiles[j]
-            hidden_products, mx_products = [], []
-            for c in range(CELLS):
-                ph = psum.tile([P, NET], F32, tag="ph", bufs=2)
-                for kt in range(K_TILES):
-                    nc.tensor.matmul(
-                        ph[:],
-                        lhsT=ht_sb[:, i, kt, :],
-                        rhs=wh_t[:, kt, c * NET : (c + 1) * NET],
-                        start=(kt == 0),
-                        stop=(kt == K_TILES - 1),
-                    )
-                hidden_products.append(ph)
+        def add_bias(t, c):
+            if c == 0:
+                net = results.tile([P, CELLS, NET], F32)
+                net_tiles[t] = net
+            nc.vector.tensor_tensor(
+                out=net_tiles[t][:, c, :], in0=ph_tiles[(t, c)][:], in1=bias[:, c, :], op=ADD
+            )
+
+        def mx_product(t):
+            codes, planes = code_tiles[t], plane_tiles[t]
             for c in range(CELLS):
                 px = psum.tile([P, NET], F32, tag="px", bufs=3)
                 for g in range(PASSES):
@@ -122,23 +138,29 @@ def tile_compute_gate_t_e_kernel(
                         start=(g == 0),
                         stop=(g == PASSES - 1),
                     )
-                mx_products.append(px)
-            net = results.tile([P, CELLS, NET], F32)
-            for c in range(CELLS):
-                nc.vector.tensor_tensor(
-                    out=net[:, c, :], in0=hidden_products[c][:], in1=bias[:, c, :], op=ADD
-                )
-            for c in range(CELLS):
-                nc.vector.tensor_tensor(
-                    out=net[:, c, :], in0=mx_products[c][:], in1=net[:, c, :], op=ADD
-                )
-            t = j * ROUND + i
+                px_tiles[(t, c)] = px
+
+        def add_mx(t, c):
+            nc.vector.tensor_tensor(
+                out=net_tiles[t][:, c, :], in0=px_tiles[(t, c)][:], in1=net_tiles[t][:, c, :], op=ADD
+            )
+
+        def finish_gate(t):
             gate = results.tile([P, CELLS, HID], F32)
-            nc.scalar.activation(out=gate[:], in_=net[:, :, 0:HID], func=SIGMOID)
+            nc.scalar.activation(out=gate[:], in_=net_tiles[t][:, :, 0:HID], func=SIGMOID)
             nc.sync.dma_start(out=gate_rows[:, t, :, :], in_=gate[:])
+
+        def finish_cell(t):
             cell = results.tile([P, CELLS, HID], F32)
-            nc.scalar.activation(out=cell[:], in_=net[:, :, HID:NET], func=TANH)
+            nc.scalar.activation(out=cell[:], in_=net_tiles[t][:, :, HID:NET], func=TANH)
             nc.sync.dma_start(out=cell_rows[:, t, :, :], in_=cell[:])
+
+        def flip_run(t):
+            for s in range(2 * PASSES):
+                flip_x(t, s)
+            for kt in range(K_TILES):
+                flip_h(t, kt)
+            copy_flipped(t)
 
         ident_f32 = consts.tile([P, P], F32)
         make_identity(nc, ident_f32[:])
@@ -151,7 +173,7 @@ def tile_compute_gate_t_e_kernel(
         w_planes = consts.tile([P, GROUPS, NET], U8, align_bytes=64)
         nc.vector.memset(w_planes[:].rearrange("p g n -> p (g n)").bitcast(I32), 0)
 
-        load_round(0)
+        load(0)
         nc.sync.dma_start(out=bias_row[0:1, :], in_=bx.rearrange("(o c) n -> o (c n)", o=1))
         for quadrant in range(4):
             nc.sync.dma_start(
@@ -166,8 +188,8 @@ def tile_compute_gate_t_e_kernel(
         nc.sync.dma_start(
             out=w_words[:].bitcast(I32), in_=Wx_words.rearrange("g p b -> p g b").bitcast(I32)
         )
-        for j in range(1, LOOKAHEAD):
-            load_round(j)
+        for j in range(1, LOADS_AHEAD):
+            load(j)
 
         bias = consts.tile([P, CELLS, NET], F32)
         for c in range(CELLS):
@@ -181,7 +203,8 @@ def tile_compute_gate_t_e_kernel(
             )
             nc.vector.tensor_copy(out=bias[:, c, :], in_=spread[:])
 
-        transpose_round(0)
+        flip_run(0)
+        flip_run(1)
 
         wh_t = consts.tile([P, K_TILES, CELLS * NET], BF16)
         for kt in range(K_TILES):
@@ -194,15 +217,41 @@ def tile_compute_gate_t_e_kernel(
                 )
             nc.vector.tensor_copy(out=wh_t[:, kt, :], in_=flipped[:])
 
-        for i in range(ROUND):
-            quantise_tile(0, i)
+        flip_run(2)
+        quantise(0)
+        for s in range(CELLS * K_TILES):
+            hidden_pass(0, s)
+        for c in range(CELLS):
+            add_bias(0, c)
 
-        for j in range(ROUNDS):
-            if j + LOOKAHEAD < ROUNDS:
-                load_round(j + LOOKAHEAD)
-            if j + 1 < ROUNDS:
-                transpose_round(j + 1)
-            for i in range(ROUND):
-                gates_tile(j, i)
-                if j + 1 < ROUNDS:
-                    quantise_tile(j + 1, i)
+        for t in range(TILES):
+            if t % LOAD == 0 and t // LOAD + LOADS_AHEAD < LOADS:
+                load(t // LOAD + LOADS_AHEAD)
+            ahead, flip = t + HIDDEN_AHEAD, t + FLIP_AHEAD
+            between = [[], [], []]
+            if flip < TILES:
+                between = [[("x", 0), ("h", 0)], [("x", 1), ("h", 1)], [("x", 2), ("x", 3)]]
+            for s in range(CELLS * K_TILES):
+                if ahead < TILES:
+                    hidden_pass(ahead, s)
+                if s < len(between):
+                    for kind, number in between[s]:
+                        if kind == "x":
+                            flip_x(flip, number)
+                        else:
+                            flip_h(flip, number)
+            if ahead < TILES:
+                add_bias(ahead, 0)
+                quantise(ahead)
+                add_bias(ahead, 1)
+            if t > 0:
+                finish_gate(t - 1)
+            if flip < TILES:
+                copy_flipped(flip)
+            if t > 0:
+                finish_cell(t - 1)
+            mx_product(t)
+            for c in range(CELLS):
+                add_mx(t, c)
+        finish_gate(TILES - 1)
+        finish_cell(TILES - 1)

@@ -26,7 +26,7 @@ TILES = BATCH // P
 LOAD = 2
 LOADS = TILES // LOAD
 LOADS_AHEAD = 4
-FLIP_AHEAD = 3
+FLIP_AHEAD = 2
 HIDDEN_AHEAD = 1
 
 FLOPS = 2 * BATCH * CELLS * NET * (IN + HID)
@@ -46,7 +46,7 @@ def tile_compute_gate_t_e_kernel(
         consts = ctx.enter_context(tc.tile_pool(name="consts", bufs=1))
         stream = ctx.enter_context(tc.tile_pool(name="stream", bufs=LOADS_AHEAD + 2))
         work = ctx.enter_context(tc.tile_pool(name="work", bufs=FLIP_AHEAD + 1))
-        results = ctx.enter_context(tc.tile_pool(name="results", bufs=4))
+        results = ctx.enter_context(tc.tile_pool(name="results", bufs=HIDDEN_AHEAD + 4))
         psum = ctx.enter_context(tc.psum_pool(name="psum", bufs=1))
 
         x_tiles, h_tiles = {}, {}
@@ -102,6 +102,8 @@ def tile_compute_gate_t_e_kernel(
                 in_=xt_tiles[t][:].rearrange("p (g u) r -> p g r u", u=2),
             )
             grouped_tiles[t] = grouped
+
+        def copy_flipped_hidden(t):
             ht_sb = work.tile([P, K_TILES, P], BF16)
             nc.scalar.copy(out=ht_sb[:], in_=ht_tiles[t][:])
             ht_sb_tiles[t] = ht_sb
@@ -155,13 +157,6 @@ def tile_compute_gate_t_e_kernel(
             nc.scalar.activation(out=cell[:], in_=net_tiles[t][:, :, HID:NET], func=TANH)
             nc.sync.dma_start(out=cell_rows[:, t, :, :], in_=cell[:])
 
-        def flip_run(t):
-            for s in range(2 * PASSES):
-                flip_x(t, s)
-            for kt in range(K_TILES):
-                flip_h(t, kt)
-            copy_flipped(t)
-
         ident_f32 = consts.tile([P, P], F32)
         make_identity(nc, ident_f32[:])
         ident_bf16 = consts.tile([P, P], BF16)
@@ -173,8 +168,15 @@ def tile_compute_gate_t_e_kernel(
         w_planes = consts.tile([P, GROUPS, NET], U8, align_bytes=64)
         nc.vector.memset(w_planes[:].rearrange("p g n -> p (g n)").bitcast(I32), 0)
 
-        load(0)
+        x_sb = stream.tile([P, LOAD, IN], BF16)
+        h_sb = stream.tile([P, LOAD, HID], BF16)
+        x_tiles[0], h_tiles[0] = x_sb, h_sb
+        nc.sync.dma_start(out=h_sb[:], in_=h_rows[:, 0:LOAD, :])
         nc.sync.dma_start(out=bias_row[0:1, :], in_=bx.rearrange("(o c) n -> o (c n)", o=1))
+        wh_rows = consts.tile([P, CELLS, NET // P, HID], BF16)
+        for c in range(CELLS):
+            nc.sync.dma_start(out=wh_rows[:, c, :, :], in_=Wh[c].rearrange("(b p) k -> p b k", p=P))
+        nc.sync.dma_start(out=x_sb[:, 0, :], in_=x_rows[:, 0, :])
         for quadrant in range(4):
             nc.sync.dma_start(
                 out=w_planes[32 * quadrant : 32 * quadrant + 4, :, :].bitcast(I32),
@@ -182,14 +184,18 @@ def tile_compute_gate_t_e_kernel(
                 .rearrange("g r n -> r g n")
                 .bitcast(I32),
             )
-        wh_rows = consts.tile([P, CELLS * NET // P, HID], BF16)
-        nc.sync.dma_start(out=wh_rows[:], in_=Wh.rearrange("c (b p) k -> p (c b) k", p=P))
         w_words = consts.tile([P, GROUPS, 2 * NET], U8, align_bytes=64)
         nc.sync.dma_start(
             out=w_words[:].bitcast(I32), in_=Wx_words.rearrange("g p b -> p g b").bitcast(I32)
         )
+        nc.sync.dma_start(out=x_sb[:, 1, :], in_=x_rows[:, 1, :])
         for j in range(1, LOADS_AHEAD):
             load(j)
+
+        for t in range(FLIP_AHEAD):
+            for kt in range(K_TILES):
+                flip_h(t, kt)
+            copy_flipped_hidden(t)
 
         bias = consts.tile([P, CELLS, NET], F32)
         for c in range(CELLS):
@@ -203,26 +209,33 @@ def tile_compute_gate_t_e_kernel(
             )
             nc.vector.tensor_copy(out=bias[:, c, :], in_=spread[:])
 
-        flip_run(0)
-        flip_run(1)
-
         wh_t = consts.tile([P, K_TILES, CELLS * NET], BF16)
-        for kt in range(K_TILES):
-            flipped = psum.tile([P, CELLS * NET], BF16, tag="ph", bufs=2)
-            for b in range(CELLS * NET // P):
-                nc.tensor.transpose(
-                    flipped[:, b * P : (b + 1) * P],
-                    wh_rows[:, b, kt * P : (kt + 1) * P],
-                    ident_bf16[:],
-                )
-            nc.vector.tensor_copy(out=wh_t[:, kt, :], in_=flipped[:])
+        for c in range(CELLS):
+            flipped = psum.tile([P, K_TILES, NET], BF16, tag="ph", bufs=2)
+            for kt in range(K_TILES):
+                for b in range(NET // P):
+                    nc.tensor.transpose(
+                        flipped[:, kt, b * P : (b + 1) * P],
+                        wh_rows[:, c, b, kt * P : (kt + 1) * P],
+                        ident_bf16[:],
+                    )
+            if c == 0:
+                nc.scalar.copy(out=wh_t[:, :, 0:NET], in_=flipped[:])
+            else:
+                nc.vector.tensor_copy(out=wh_t[:, :, NET : 2 * NET], in_=flipped[:])
 
-        flip_run(2)
-        quantise(0)
+        for s in range(2 * PASSES):
+            flip_x(0, s)
+        copy_flipped(0)
         for s in range(CELLS * K_TILES):
             hidden_pass(0, s)
         for c in range(CELLS):
             add_bias(0, c)
+        for t in range(1, FLIP_AHEAD):
+            for s in range(2 * PASSES):
+                flip_x(t, s)
+            copy_flipped(t)
+        quantise(0)
 
         for t in range(TILES):
             if t % LOAD == 0 and t // LOAD + LOADS_AHEAD < LOADS:
@@ -242,11 +255,14 @@ def tile_compute_gate_t_e_kernel(
                             flip_h(flip, number)
             if ahead < TILES:
                 add_bias(ahead, 0)
-                quantise(ahead)
+            if t + 1 < TILES:
+                quantise(t + 1)
+            if ahead < TILES:
                 add_bias(ahead, 1)
             if t > 0:
                 finish_gate(t - 1)
             if flip < TILES:
+                copy_flipped_hidden(flip)
                 copy_flipped(flip)
             if t > 0:
                 finish_cell(t - 1)

@@ -157,6 +157,21 @@ def tile_compute_gate_t_e_kernel(
             nc.scalar.activation(out=cell[:], in_=net_tiles[t][:, :, HID:NET], func=TANH)
             nc.sync.dma_start(out=cell_rows[:, t, :, :], in_=cell[:])
 
+        def finish_in_halves(t, c):
+            net, px = net_tiles[t], px_tiles[(t, c)]
+            nc.vector.tensor_tensor(
+                out=net[:, c, 0:HID], in0=px[:, 0:HID], in1=net[:, c, 0:HID], op=ADD
+            )
+            gate = results.tile([P, CELLS, HID], F32)
+            nc.scalar.activation(out=gate[:, c, :], in_=net[:, c, 0:HID], func=SIGMOID)
+            nc.sync.dma_start(out=gate_rows[:, t, c, :], in_=gate[:, c, :])
+            nc.vector.tensor_tensor(
+                out=net[:, c, HID:NET], in0=px[:, HID:NET], in1=net[:, c, HID:NET], op=ADD
+            )
+            cell = results.tile([P, CELLS, HID], F32)
+            nc.scalar.activation(out=cell[:, c, :], in_=net[:, c, HID:NET], func=TANH)
+            nc.sync.dma_start(out=cell_rows[:, t, c, :], in_=cell[:, c, :])
+
         ident_f32 = consts.tile([P, P], F32)
         make_identity(nc, ident_f32[:])
         ident_bf16 = consts.tile([P, P], BF16)
@@ -237,7 +252,7 @@ def tile_compute_gate_t_e_kernel(
             copy_flipped(t)
         quantise(0)
 
-        for t in range(TILES):
+        for t in range(TILES - 2):
             if t % LOAD == 0 and t // LOAD + LOADS_AHEAD < LOADS:
                 load(t // LOAD + LOADS_AHEAD)
             ahead, flip = t + HIDDEN_AHEAD, t + FLIP_AHEAD
@@ -269,5 +284,20 @@ def tile_compute_gate_t_e_kernel(
             mx_product(t)
             for c in range(CELLS):
                 add_mx(t, c)
-        finish_gate(TILES - 1)
-        finish_cell(TILES - 1)
+
+        last = TILES - 1
+        quantise(last)
+        finish_gate(last - 2)
+        finish_cell(last - 2)
+        mx_product(last - 1)
+        for c in range(CELLS):
+            add_mx(last - 1, c)
+        finish_gate(last - 1)
+        finish_cell(last - 1)
+        for s in range(CELLS * K_TILES):
+            hidden_pass(last, s)
+        for c in range(CELLS):
+            add_bias(last, c)
+        mx_product(last)
+        for c in range(CELLS):
+            finish_in_halves(last, c)

@@ -82,6 +82,9 @@ def tile_compute_gate_t_e_kernel(
                 ident_bf16[:],
             )
 
+        def aside(t, c):
+            return c == 1 and t % 2 == 1
+
         def hidden_pass(t, s):
             c, kt = divmod(s, K_TILES)
             if kt == 0:
@@ -92,8 +95,16 @@ def tile_compute_gate_t_e_kernel(
                 lhsT=ht_sb_tiles[t][:, kt, :],
                 rhs=wh_t[:, kt, c * NET : (c + 1) * NET],
                 start=(kt == 0),
-                stop=(kt == K_TILES - 1),
+                stop=(kt == K_TILES - 1 and not aside(t, c)),
             )
+            if kt == K_TILES - 1 and aside(t, c):
+                nc.tensor.matmul(
+                    ph_tiles[(t, c)][:],
+                    lhsT=ones[:],
+                    rhs=bias_row[:, c * NET : (c + 1) * NET],
+                    start=False,
+                    stop=True,
+                )
 
         def copy_flipped(t):
             grouped = work.tile([P, PASSES, P, PACK], BF16, align_bytes=64)
@@ -122,9 +133,12 @@ def tile_compute_gate_t_e_kernel(
             if c == 0:
                 net = results.tile([P, CELLS, NET], F32)
                 net_tiles[t] = net
-            nc.vector.tensor_tensor(
-                out=net_tiles[t][:, c, :], in0=ph_tiles[(t, c)][:], in1=bias[:, c, :], op=ADD
-            )
+            if aside(t, c):
+                nc.scalar.copy(out=net_tiles[t][:, c, :], in_=ph_tiles[(t, c)][:])
+            else:
+                nc.vector.tensor_tensor(
+                    out=net_tiles[t][:, c, :], in0=ph_tiles[(t, c)][:], in1=bias[:, c, :], op=ADD
+                )
 
         def mx_product(t):
             codes, planes = code_tiles[t], plane_tiles[t]
@@ -272,13 +286,15 @@ def tile_compute_gate_t_e_kernel(
                 add_bias(ahead, 0)
             if t + 1 < TILES:
                 quantise(t + 1)
-            if ahead < TILES:
+            if ahead < TILES and not aside(ahead, 1):
                 add_bias(ahead, 1)
             if t > 0:
                 finish_gate(t - 1)
             if flip < TILES:
                 copy_flipped_hidden(flip)
                 copy_flipped(flip)
+            if ahead < TILES and aside(ahead, 1):
+                add_bias(ahead, 1)
             if t > 0:
                 finish_cell(t - 1)
             mx_product(t)

@@ -83,7 +83,7 @@ def tile_compute_gate_t_e_kernel(
             )
 
         def aside(t, c):
-            return c == 1 and t % 2 == 1
+            return c == 1 and t % 3 == 1
 
         def hidden_pass(t, s):
             c, kt = divmod(s, K_TILES)

@@ -288,14 +288,14 @@ def tile_compute_gate_t_e_kernel(
                 quantise(t + 1)
             if ahead < TILES and not aside(ahead, 1):
                 add_bias(ahead, 1)
-            if t > 0:
-                finish_gate(t - 1)
             if flip < TILES:
                 copy_flipped_hidden(flip)
+            if flip < TILES:
                 copy_flipped(flip)
             if ahead < TILES and aside(ahead, 1):
                 add_bias(ahead, 1)
             if t > 0:
+                finish_gate(t - 1)
                 finish_cell(t - 1)
             mx_product(t)
             for c in range(CELLS):

@@ -85,26 +85,33 @@ def tile_compute_gate_t_e_kernel(
         def aside(t, c):
             return c == 1 and t % 3 == 1
 
-        def hidden_pass(t, s):
+        def hidden_pass(t, s, first=0, width=NET):
             c, kt = divmod(s, K_TILES)
             if kt == 0:
                 ph = psum.tile([P, NET], F32, tag="ph", bufs=2)
                 ph_tiles[(t, c)] = ph
             nc.tensor.matmul(
-                ph_tiles[(t, c)][:],
+                ph_tiles[(t, c)][:, first : first + width],
                 lhsT=ht_sb_tiles[t][:, kt, :],
-                rhs=wh_t[:, kt, c * NET : (c + 1) * NET],
+                rhs=wh_t[:, kt, c * NET + first : c * NET + first + width],
                 start=(kt == 0),
-                stop=(kt == K_TILES - 1 and not aside(t, c)),
+                stop=(kt == K_TILES - 1 and first + width == NET and not aside(t, c)),
             )
-            if kt == K_TILES - 1 and aside(t, c):
-                nc.tensor.matmul(
-                    ph_tiles[(t, c)][:],
-                    lhsT=ones[:],
-                    rhs=bias_row[:, c * NET : (c + 1) * NET],
-                    start=False,
-                    stop=True,
-                )
+
+        def bias_pass(t, c):
+            nc.tensor.matmul(
+                ph_tiles[(t, c)][:],
+                lhsT=ones[:],
+                rhs=bias_row[:, c * NET : (c + 1) * NET],
+                start=False,
+                stop=True,
+            )
+
+        def hidden_product(t):
+            for s in range(CELLS * K_TILES):
+                hidden_pass(t, s)
+            if aside(t, 1):
+                bias_pass(t, 1)
 
         def copy_flipped(t):
             grouped = work.tile([P, PASSES, P, PACK], BF16, align_bytes=64)
@@ -256,8 +263,7 @@ def tile_compute_gate_t_e_kernel(
         for s in range(2 * PASSES):
             flip_x(0, s)
         copy_flipped(0)
-        for s in range(CELLS * K_TILES):
-            hidden_pass(0, s)
+        hidden_product(0)
         for c in range(CELLS):
             add_bias(0, c)
         for t in range(1, FLIP_AHEAD):
@@ -270,18 +276,25 @@ def tile_compute_gate_t_e_kernel(
             if t % LOAD == 0 and t // LOAD + LOADS_AHEAD < LOADS:
                 load(t // LOAD + LOADS_AHEAD)
             ahead, flip = t + HIDDEN_AHEAD, t + FLIP_AHEAD
-            between = [[], [], []]
             if flip < TILES:
-                between = [[("x", 0), ("h", 0)], [("x", 1), ("h", 1)], [("x", 2), ("x", 3)]]
-            for s in range(CELLS * K_TILES):
-                if ahead < TILES:
-                    hidden_pass(ahead, s)
-                if s < len(between):
-                    for kind, number in between[s]:
-                        if kind == "x":
-                            flip_x(flip, number)
-                        else:
-                            flip_h(flip, number)
+                hidden_pass(ahead, 0)
+                flip_x(flip, 0)
+                flip_h(flip, 0)
+                hidden_pass(ahead, 1)
+                flip_x(flip, 1)
+                flip_h(flip, 1)
+                hidden_pass(ahead, 2)
+                flip_x(flip, 2)
+                if aside(ahead, 1):
+                    hidden_pass(ahead, 3)
+                    flip_x(flip, 3)
+                    bias_pass(ahead, 1)
+                else:
+                    hidden_pass(ahead, 3, 0, HID)
+                    flip_x(flip, 3)
+                    hidden_pass(ahead, 3, HID, HID)
+            elif ahead < TILES:
+                hidden_product(ahead)
             if ahead < TILES:
                 add_bias(ahead, 0)
             if t + 1 < TILES:
@@ -310,8 +323,7 @@ def tile_compute_gate_t_e_kernel(
             add_mx(last - 1, c)
         finish_gate(last - 1)
         finish_cell(last - 1)
-        for s in range(CELLS * K_TILES):
-            hidden_pass(last, s)
+        hidden_product(last)
         for c in range(CELLS):
             add_bias(last, c)
         mx_product(last)

@@ -28,6 +28,7 @@ LOADS = TILES // LOAD
 LOADS_AHEAD = 4
 FLIP_AHEAD = 2
 HIDDEN_AHEAD = 1
+WARM_UP = 12
 
 FLOPS = 2 * BATCH * CELLS * NET * (IN + HID)
 
@@ -83,7 +84,7 @@ def tile_compute_gate_t_e_kernel(
             )
 
         def aside(t, c):
-            return c == 1 and t % 3 == 1
+            return c == 1 and t % 2 == 1 and t < TILES - 1
 
         def hidden_pass(t, s, first=0, width=NET):
             c, kt = divmod(s, K_TILES)
@@ -208,10 +209,10 @@ def tile_compute_gate_t_e_kernel(
         h_sb = stream.tile([P, LOAD, HID], BF16)
         x_tiles[0], h_tiles[0] = x_sb, h_sb
         nc.sync.dma_start(out=h_sb[:], in_=h_rows[:, 0:LOAD, :])
-        nc.sync.dma_start(out=bias_row[0:1, :], in_=bx.rearrange("(o c) n -> o (c n)", o=1))
         wh_rows = consts.tile([P, CELLS, NET // P, HID], BF16)
         for c in range(CELLS):
             nc.sync.dma_start(out=wh_rows[:, c, :, :], in_=Wh[c].rearrange("(b p) k -> p b k", p=P))
+        nc.sync.dma_start(out=bias_row[0:1, :], in_=bx.rearrange("(o c) n -> o (c n)", o=1))
         nc.sync.dma_start(out=x_sb[:, 0, :], in_=x_rows[:, 0, :])
         for quadrant in range(4):
             nc.sync.dma_start(
@@ -228,22 +229,14 @@ def tile_compute_gate_t_e_kernel(
         for j in range(1, LOADS_AHEAD):
             load(j)
 
+        for i in range(WARM_UP):
+            idle = psum.tile([P, NET], F32, tag="px", bufs=3)
+            nc.tensor.matmul(idle[:, 0:P], lhsT=ones[:], rhs=ones[:], start=True, stop=True)
+
         for t in range(FLIP_AHEAD):
             for kt in range(K_TILES):
                 flip_h(t, kt)
             copy_flipped_hidden(t)
-
-        bias = consts.tile([P, CELLS, NET], F32)
-        for c in range(CELLS):
-            spread = psum.tile([P, NET], F32, tag="px", bufs=3)
-            nc.tensor.matmul(
-                spread[:],
-                lhsT=ones[:],
-                rhs=bias_row[:, c * NET : (c + 1) * NET],
-                start=True,
-                stop=True,
-            )
-            nc.vector.tensor_copy(out=bias[:, c, :], in_=spread[:])
 
         wh_t = consts.tile([P, K_TILES, CELLS * NET], BF16)
         for c in range(CELLS):
@@ -259,6 +252,18 @@ def tile_compute_gate_t_e_kernel(
                 nc.scalar.copy(out=wh_t[:, :, 0:NET], in_=flipped[:])
             else:
                 nc.vector.tensor_copy(out=wh_t[:, :, NET : 2 * NET], in_=flipped[:])
+
+        bias = consts.tile([P, CELLS, NET], F32)
+        for c in range(CELLS):
+            spread = psum.tile([P, NET], F32, tag="px", bufs=3)
+            nc.tensor.matmul(
+                spread[:],
+                lhsT=ones[:],
+                rhs=bias_row[:, c * NET : (c + 1) * NET],
+                start=True,
+                stop=True,
+            )
+            nc.vector.tensor_copy(out=bias[:, c, :], in_=spread[:])
 
         for s in range(2 * PASSES):
             flip_x(0, s)

from contextlib import ExitStack

import concourse.mybir as mybir
from concourse.masks import make_identity

F32 = mybir.dt.float32
BF16 = mybir.dt.bfloat16
I32 = mybir.dt.int32
U32 = mybir.dt.uint32
U8 = mybir.dt.uint8
FP8X4 = mybir.dt.float8_e4m3fn_x4
FP4X4 = mybir.dt.float4_e2m1fn_x4
ADD = mybir.AluOpType.add
SIGMOID = mybir.ActivationFunctionType.Sigmoid
TANH = mybir.ActivationFunctionType.Tanh

P = 128
BATCH, IN, HID, CELLS = 4096, 1024, 256, 2
NET = 2 * HID
PACK = 4
K_PASS = P * PACK
PASSES = IN // K_PASS
GROUPS = CELLS * PASSES
K_TILES = HID // P
TILES = BATCH // P
LOAD = 2
LOADS = TILES // LOAD
LOADS_AHEAD = 4
FLIP_AHEAD = 2
HIDDEN_AHEAD = 1
WARM_UP = 12

FLOPS = 2 * BATCH * CELLS * NET * (IN + HID)


def tile_compute_gate_t_e_kernel(
    tc, input_word, hidden_states, Wx_words, Wx_scales, bx, Wh, out_0, out_1
):
    nc = tc.nc
    x_rows = input_word.rearrange("(p t) k -> p t k", t=TILES)
    h_rows = hidden_states.rearrange("(p t) k -> p t k", t=TILES)
    cell_rows = out_0.rearrange("(p t) c n -> p t c n", t=TILES)
    gate_rows = out_1.rearrange("(p t) c n -> p t c n", t=TILES)

    with ExitStack() as ctx:
        ctx.enter_context(tc.manual_schedule())
        consts = ctx.enter_context(tc.tile_pool(name="consts", bufs=1))
        stream = ctx.enter_context(tc.tile_pool(name="stream", bufs=LOADS_AHEAD + 2))
        work = ctx.enter_context(tc.tile_pool(name="work", bufs=FLIP_AHEAD + 1))
        results = ctx.enter_context(tc.tile_pool(name="results", bufs=HIDDEN_AHEAD + 4))
        psum = ctx.enter_context(tc.psum_pool(name="psum", bufs=1))

        x_tiles, h_tiles = {}, {}
        xt_tiles, ht_tiles = {}, {}
        grouped_tiles, code_tiles, plane_tiles, ht_sb_tiles = {}, {}, {}, {}
        ph_tiles, px_tiles, net_tiles = {}, {}, {}

        def load(j):
            first = j * LOAD
            x_sb = stream.tile([P, LOAD, IN], BF16)
            nc.sync.dma_start(out=x_sb[:], in_=x_rows[:, first : first + LOAD, :])
            h_sb = stream.tile([P, LOAD, HID], BF16)
            nc.sync.dma_start(out=h_sb[:], in_=h_rows[:, first : first + LOAD, :])
            x_tiles[j], h_tiles[j] = x_sb, h_sb

        def flip_x(t, s):
            if s == 0:
                xt = psum.tile([P, PASSES * 2, P], F32, tag="xt", bufs=2)
                xt_tiles[t] = xt
            g, u = divmod(s, 2)
            words = x_tiles[t // LOAD][:, t % LOAD, :].bitcast(F32)
            nc.tensor.transpose(
                xt_tiles[t][:, s, :], words[:, 256 * g + u : 256 * (g + 1) : 2], ident_f32[:]
            )

        def flip_h(t, kt):
            if kt == 0:
                ht = psum.tile([P, K_TILES, P], BF16, tag="ht", bufs=1)
                ht_tiles[t] = ht
            nc.tensor.transpose(
                ht_tiles[t][:, kt, :],
                h_tiles[t // LOAD][:, t % LOAD, kt * P : (kt + 1) * P],
                ident_bf16[:],
            )

        def aside(t, c):
            return c == 1 and t % 2 == 1 and t < TILES - 1

        def hidden_pass(t, s, first=0, width=NET):
            c, kt = divmod(s, K_TILES)
            if kt == 0:
                ph = psum.tile([P, NET], F32, tag="ph", bufs=2)
                ph_tiles[(t, c)] = ph
            nc.tensor.matmul(
                ph_tiles[(t, c)][:, first : first + width],
                lhsT=ht_sb_tiles[t][:, kt, :],
                rhs=wh_t[:, kt, c * NET + first : c * NET + first + width],
                start=(kt == 0),
                stop=(kt == K_TILES - 1 and first + width == NET and not aside(t, c)),
            )

        def bias_pass(t, c):
            nc.tensor.matmul(
                ph_tiles[(t, c)][:],
                lhsT=ones[:],
                rhs=bias_row[:, c * NET : (c + 1) * NET],
                start=False,
                stop=True,
            )

        def hidden_product(t):
            for s in range(CELLS * K_TILES):
                hidden_pass(t, s)
            if aside(t, 1):
                bias_pass(t, 1)

        def copy_flipped(t):
            grouped = work.tile([P, PASSES, P, PACK], BF16, align_bytes=64)
            nc.scalar.copy(
                out=grouped[:].bitcast(F32),
                in_=xt_tiles[t][:].rearrange("p (g u) r -> p g r u", u=2),
            )
            grouped_tiles[t] = grouped

        def copy_flipped_hidden(t):
            ht_sb = work.tile([P, K_TILES, P], BF16)
            nc.scalar.copy(out=ht_sb[:], in_=ht_tiles[t][:])
            ht_sb_tiles[t] = ht_sb

        def quantise(t):
            codes = work.tile([P, PASSES * P], U32, align_bytes=64)
            planes = work.tile([P, PASSES * P], U8, align_bytes=64)
            nc.vector.quantize_mx(
                out=codes[:].bitcast(FP8X4),
                scales=planes[:],
                in_=grouped_tiles[t][:].rearrange("p g r t -> p (g r t)"),
            )
            code_tiles[t], plane_tiles[t] = codes, planes

        def add_bias(t, c):
            if c == 0:
                net = results.tile([P, CELLS, NET], F32)
                net_tiles[t] = net
            if aside(t, c):
                nc.scalar.copy(out=net_tiles[t][:, c, :], in_=ph_tiles[(t, c)][:])
            else:
                nc.vector.tensor_tensor(
                    out=net_tiles[t][:, c, :], in0=ph_tiles[(t, c)][:], in1=bias[:, c, :], op=ADD
                )

        def mx_product(t):
            codes, planes = code_tiles[t], plane_tiles[t]
            for c in range(CELLS):
                px = psum.tile([P, NET], F32, tag="px", bufs=3)
                for g in range(PASSES):
                    nc.tensor.matmul_mx(
                        out=px[:],
                        lhsT=codes[:, g * P : (g + 1) * P].bitcast(FP8X4),
                        lhsT_scale=planes[:, g * P : (g + 1) * P],
                        rhs=w_words[:, c * PASSES + g, :].bitcast(FP4X4),
                        rhs_scale=w_planes[:, c * PASSES + g, :],
                        start=(g == 0),
                        stop=(g == PASSES - 1),
                    )
                px_tiles[(t, c)] = px

        def add_mx(t, c):
            nc.vector.tensor_tensor(
                out=net_tiles[t][:, c, :], in0=px_tiles[(t, c)][:], in1=net_tiles[t][:, c, :], op=ADD
            )

        def finish_gate(t):
            gate = results.tile([P, CELLS, HID], F32)
            nc.scalar.activation(out=gate[:], in_=net_tiles[t][:, :, 0:HID], func=SIGMOID)
            nc.sync.dma_start(out=gate_rows[:, t, :, :], in_=gate[:])

        def finish_cell(t):
            cell = results.tile([P, CELLS, HID], F32)
            nc.scalar.activation(out=cell[:], in_=net_tiles[t][:, :, HID:NET], func=TANH)
            nc.sync.dma_start(out=cell_rows[:, t, :, :], in_=cell[:])

        def finish_in_halves(t, c):
            net, px = net_tiles[t], px_tiles[(t, c)]
            nc.vector.tensor_tensor(
                out=net[:, c, 0:HID], in0=px[:, 0:HID], in1=net[:, c, 0:HID], op=ADD
            )
            gate = results.tile([P, CELLS, HID], F32)
            nc.scalar.activation(out=gate[:, c, :], in_=net[:, c, 0:HID], func=SIGMOID)
            nc.sync.dma_start(out=gate_rows[:, t, c, :], in_=gate[:, c, :])
            nc.vector.tensor_tensor(
                out=net[:, c, HID:NET], in0=px[:, HID:NET], in1=net[:, c, HID:NET], op=ADD
            )
            cell = results.tile([P, CELLS, HID], F32)
            nc.scalar.activation(out=cell[:, c, :], in_=net[:, c, HID:NET], func=TANH)
            nc.sync.dma_start(out=cell_rows[:, t, c, :], in_=cell[:, c, :])

        ident_f32 = consts.tile([P, P], F32)
        make_identity(nc, ident_f32[:])
        ident_bf16 = consts.tile([P, P], BF16)
        make_identity(nc, ident_bf16[:])
        ones = consts.tile([P, P], BF16)
        nc.vector.memset(ones[:], 1.0)
        bias_row = consts.tile([P, CELLS * NET], BF16)
        nc.vector.memset(bias_row[:], 0.0)
        w_planes = consts.tile([P, GROUPS, NET], U8, align_bytes=64)
        nc.vector.memset(w_planes[:].rearrange("p g n -> p (g n)").bitcast(I32), 0)

        x_sb = stream.tile([P, LOAD, IN], BF16)
        h_sb = stream.tile([P, LOAD, HID], BF16)
        x_tiles[0], h_tiles[0] = x_sb, h_sb
        nc.sync.dma_start(out=h_sb[:], in_=h_rows[:, 0:LOAD, :])
        wh_rows = consts.tile([P, CELLS, NET // P, HID], BF16)
        for c in range(CELLS):
            nc.sync.dma_start(out=wh_rows[:, c, :, :], in_=Wh[c].rearrange("(b p) k -> p b k", p=P))
        nc.sync.dma_start(out=bias_row[0:1, :], in_=bx.rearrange("(o c) n -> o (c n)", o=1))
        nc.sync.dma_start(out=x_sb[:, 0, :], in_=x_rows[:, 0, :])
        for quadrant in range(4):
            nc.sync.dma_start(
                out=w_planes[32 * quadrant : 32 * quadrant + 4, :, :].bitcast(I32),
                in_=Wx_scales[:, 4 * quadrant : 4 * quadrant + 4, :]
                .rearrange("g r n -> r g n")
                .bitcast(I32),
            )
        w_words = consts.tile([P, GROUPS, 2 * NET], U8, align_bytes=64)
        nc.sync.dma_start(
            out=w_words[:].bitcast(I32), in_=Wx_words.rearrange("g p b -> p g b").bitcast(I32)
        )
        nc.sync.dma_start(out=x_sb[:, 1, :], in_=x_rows[:, 1, :])
        for j in range(1, LOADS_AHEAD):
            load(j)

        for i in range(WARM_UP):
            idle = psum.tile([P, NET], F32, tag="px", bufs=3)
            nc.tensor.matmul(idle[:, 0:P], lhsT=ones[:], rhs=ones[:], start=True, stop=True)

        for t in range(FLIP_AHEAD):
            for kt in range(K_TILES):
                flip_h(t, kt)
            copy_flipped_hidden(t)

        wh_t = consts.tile([P, K_TILES, CELLS * NET], BF16)
        for c in range(CELLS):
            flipped = psum.tile([P, K_TILES, NET], BF16, tag="ph", bufs=2)
            for kt in range(K_TILES):
                for b in range(NET // P):
                    nc.tensor.transpose(
                        flipped[:, kt, b * P : (b + 1) * P],
                        wh_rows[:, c, b, kt * P : (kt + 1) * P],
                        ident_bf16[:],
                    )
            if c == 0:
                nc.scalar.copy(out=wh_t[:, :, 0:NET], in_=flipped[:])
            else:
                nc.vector.tensor_copy(out=wh_t[:, :, NET : 2 * NET], in_=flipped[:])

        bias = consts.tile([P, CELLS, NET], F32)
        for c in range(CELLS):
            spread = psum.tile([P, NET], F32, tag="px", bufs=3)
            nc.tensor.matmul(
                spread[:],
                lhsT=ones[:],
                rhs=bias_row[:, c * NET : (c + 1) * NET],
                start=True,
                stop=True,
            )
            nc.vector.tensor_copy(out=bias[:, c, :], in_=spread[:])

        for s in range(2 * PASSES):
            flip_x(0, s)
        copy_flipped(0)
        hidden_product(0)
        for c in range(CELLS):
            add_bias(0, c)
        for t in range(1, FLIP_AHEAD):
            for s in range(2 * PASSES):
                flip_x(t, s)
            copy_flipped(t)
        quantise(0)

        for t in range(TILES - 2):
            if t % LOAD == 0 and t // LOAD + LOADS_AHEAD < LOADS:
                load(t // LOAD + LOADS_AHEAD)
            ahead, flip = t + HIDDEN_AHEAD, t + FLIP_AHEAD
            if flip < TILES:
                hidden_pass(ahead, 0)
                flip_x(flip, 0)
                flip_h(flip, 0)
                hidden_pass(ahead, 1)
                flip_x(flip, 1)
                flip_h(flip, 1)
                hidden_pass(ahead, 2)
                flip_x(flip, 2)
                if aside(ahead, 1):
                    hidden_pass(ahead, 3)
                    flip_x(flip, 3)
                    bias_pass(ahead, 1)
                else:
                    hidden_pass(ahead, 3, 0, HID)
                    flip_x(flip, 3)
                    hidden_pass(ahead, 3, HID, HID)
            elif ahead < TILES:
                hidden_product(ahead)
            if ahead < TILES:
                add_bias(ahead, 0)
            if t + 1 < TILES:
                quantise(t + 1)
            if ahead < TILES and not aside(ahead, 1):
                add_bias(ahead, 1)
            if flip < TILES:
                copy_flipped_hidden(flip)
            if flip < TILES:
                copy_flipped(flip)
            if ahead < TILES and aside(ahead, 1):
                add_bias(ahead, 1)
            if t > 0:
                finish_gate(t - 1)
                finish_cell(t - 1)
            mx_product(t)
            for c in range(CELLS):
                add_mx(t, c)

        last = TILES - 1
        quantise(last)
        finish_gate(last - 2)
        finish_cell(last - 2)
        mx_product(last - 1)
        for c in range(CELLS):
            add_mx(last - 1, c)
        finish_gate(last - 1)
        finish_cell(last - 1)
        hidden_product(last)
        for c in range(CELLS):
            add_bias(last, c)
        mx_product(last)
        for c in range(CELLS):
            finish_in_halves(last, c)
